import numpy as np
import ml_dtypes


def mxq(x, axis, fmt="e4m3"):
    dtype, down = {"e4m3": (ml_dtypes.float8_e4m3fn, 7), "e5m2": (ml_dtypes.float8_e5m2, 14)}[fmt]
    v = np.moveaxis(np.asarray(x, np.float32).astype(ml_dtypes.bfloat16).astype(np.float64), axis, -1)
    blocks = v.reshape(v.shape[:-1] + (-1, 32))
    amax = np.abs(blocks).max(-1, keepdims=True)
    byte = np.maximum(np.where(amax > 0, np.frexp(amax)[1] - 1 + 127, 0) - down, 1)
    scale = np.exp2(byte - 127.0)
    codes = (blocks / scale).astype(np.float32).astype(dtype).astype(np.float64)
    return np.moveaxis((codes * scale).reshape(v.shape), -1, axis)


WIDE = False


def mx_kscale(k):
    if not WIDE:
        return np.ones(k)
    levels = np.array([18, -18])
    if k % 512:
        return np.exp2(np.random.permutation(np.resize(levels, k // 32))).repeat(32)
    a = np.empty((k // 512, 16))
    for p in range(k // 512):
        a[p, :8] = np.random.permutation(np.resize(levels, 8))
        for g in range(8):
            far = levels[np.abs(levels - a[p, g]) >= 10]
            a[p, g + 8] = far[np.random.randint(len(far))]
    return np.exp2(a.ravel()).repeat(32)


BF16 = ml_dtypes.bfloat16


def bf(x):
    return np.asarray(x, np.float32).astype(BF16)


def f64(x):
    return np.asarray(x).astype(np.float64)


C, F, H, B, S = 2, 512, 1024, 1, 512


def setup_inputs():
    u = mx_kscale(S)
    v = mx_kscale(H)
    s = mx_kscale(S + F)
    rows = np.concatenate([np.ones(S), s[S:]])
    g = 0.3 / np.sqrt(H)
    hidden0 = bf(np.random.standard_normal((B, S, H)))
    emb0 = bf(np.random.standard_normal((C, F, H)) * 0.3)
    wk0 = bf(np.random.standard_normal((C, H, H)) * g)
    wq = bf(np.random.standard_normal((C, H, H)) * g)
    vsum = bf(np.random.standard_normal((C, B, S)))
    go = bf(np.random.standard_normal((B, C, S + F, S)) * np.exp2(np.random.randint(-6, 1, (B, C, S + F, 1))) * 0.25 / rows[:, None] * u)
    query = f64(hidden0)[None] @ f64(wq).transpose(0, 2, 1)[:, None]
    return {"hidden": bf(f64(hidden0) * v / u[:, None]),
            "emb": bf(f64(emb0) * s[S:][:, None]),
            "Wk": bf(f64(wk0) / v),
            "Wq": wq,
            "vsum": vsum,
            "query": np.asarray(query, np.float32),
            "grad_out": go}


def reference(hidden, emb, Wk, Wq, vsum, query, grad_out):
    dz2 = f64(grad_out)[0] * f64(vsum)[:, 0][:, None, :]
    dp = mxq(dz2, 2, "e5m2") @ mxq(f64(hidden)[0], 0, "e4m3")
    demb = mxq(dp[:, S:], 2, "e5m2") @ mxq(f64(Wk), 2, "e4m3").transpose(0, 2, 1)
    r = np.concatenate([f64(query)[:, 0], f64(emb)], axis=1)
    dwk = mxq(r, 1, "e4m3").transpose(0, 2, 1) @ mxq(dp, 1, "e5m2")
    return demb, dwk

@@ -1,0 +1,312 @@
+from contextlib import ExitStack
+
+import concourse.mybir as mybir
+from concourse.masks import make_identity
+
+C, S, F, H = 2, 512, 512, 1024
+FLOPS = 2 * C * ((S + F) * S * H + F * H * H + H * (S + F) * H)
+BYTES = 2 * (S * H + C * F * H + C * H * H + C * S + C * (S + F) * S) + 4 * (C * S * H + C * F * H + C * H * H)
+
+F32 = mybir.dt.float32
+BF16 = mybir.dt.bfloat16
+U32 = mybir.dt.uint32
+U8 = mybir.dt.uint8
+E4M3 = mybir.dt.float8_e4m3fn_x4
+E5M2 = mybir.dt.float8_e5m2_x4
+
+P = 128
+N = 512
+TOK, LAB = 0, 1
+STAGE = 12
+
+
+def tile_relationtagger_pa_v_kernel(tc, hidden, emb, Wk, Wq, vsum, query, grad_out, out_0, out_1):
+    nc = tc.nc
+    with ExitStack() as ctx:
+        sb = ctx.enter_context(tc.tile_pool(name="sb", bufs=1))
+        ps = ctx.enter_context(tc.psum_pool(name="ps", bufs=1))
+        ctx.enter_context(tc.manual_schedule())
+
+        taken = {}
+
+        def ring(pool, kind, depth, shape, dtype):
+            k = taken.get(kind, 0)
+            taken[kind] = k + 1
+            slot = "%s%d" % (kind, k % depth)
+            if pool is ps:
+                return pool.tile(shape, dtype, name=slot, tag=slot)
+            return pool.tile(shape, dtype, name=slot, tag=slot, align_bytes=64)
+
+        def bank():
+            return ring(ps, "bank", 8, [P, N], F32)
+
+        def packed():
+            return ring(sb, "packed", 8, [P, 4 * N], BF16)
+
+        def copy(engine, out, in_):
+            if engine is nc.scalar:
+                engine.copy(out=out, in_=in_)
+            else:
+                engine.tensor_copy(out=out, in_=in_)
+
+        V, A = nc.vector, nc.scalar
+        raw, ready, mx, dh, staged = {}, {}, {}, {}, {}
+
+        ident = sb.tile([P, P], F32, name="ident", align_bytes=64)
+        make_identity(nc, ident[:])
+        vs = sb.tile([P, C, 4], BF16, name="vs", align_bytes=64)
+
+        def load_vsum():
+            nc.scalar.dma_start(out=vs[:], in_=vsum[:, 0, :].rearrange("c (p t) -> p c t", t=4))
+
+        def load_hidden(g):
+            t = ring(sb, "raw_h", 2, [P, 4 * N], BF16)
+            raw["h", g] = t
+            nc.sync.dma_start(out=t[:].rearrange("p (t h) -> p t h", t=4),
+                              in_=hidden[0, :, g * N:(g + 1) * N].rearrange("(p t) h -> p t h", t=4))
+
+        def load_grad(c, r):
+            t = ring(sb, "raw_g", 3, [P, 4 * N], BF16)
+            raw["z", c, r] = t
+            nc.sync.dma_start(out=t[:].rearrange("q (b x) -> q b x", b=2),
+                              in_=grad_out[0, c, r * N:(r + 1) * N, :].rearrange("(b q u) j -> q b (u j)", b=2, u=2))
+
+        def load_wk(c, oh):
+            t = ring(sb, "raw_w", 2, [P, 4 * H], BF16)
+            raw["w", c, oh] = t
+            nc.sync.dma_start(out=t[:].rearrange("m (s h) -> m s h", s=4),
+                              in_=Wk[c, oh * N:(oh + 1) * N, :].rearrange("(s m) h -> m s h", s=4))
+
+        def load_emb(c):
+            t = ring(sb, "raw_e", 2, [P, 4 * H], BF16)
+            nc.sync.dma_start(out=t[:], in_=emb[c].rearrange("(p j) o -> p (j o)", j=4))
+            for oh in range(2):
+                raw["r", c, LAB, oh] = t[:].rearrange("p (e u o) -> p e u o", e=2, u=2)[:, :, :, oh * N:(oh + 1) * N]
+
+        def load_query(c, oh):
+            t = ring(sb, "raw_q", 3, [P, 4 * N], F32)
+            nc.sync.dma_start(out=t[:].rearrange("p (j o) -> p j o", j=4),
+                              in_=query[c, 0, :, oh * N:(oh + 1) * N].rearrange("(p j) o -> p j o", j=4))
+            raw["r", c, TOK, oh] = t[:].rearrange("p (e u o) -> p e u o", e=2, u=2)
+
+        def quantise(key):
+            kind = key[0]
+            depth = {"h": 2, "z": 3, "w": 4, "r": 8, "a": 6, "b": 2}[kind]
+            codes = ring(sb, "codes_" + kind, depth, [P, N], U32)
+            scales = ring(sb, "scales_" + kind, depth, [P, N], U8)
+            view = codes[:].bitcast(E5M2 if kind in "zab" else E4M3)
+            nc.vector.quantize_mx(out=view, scales=scales[:], in_=ready[key][:])
+            mx[key] = (view, scales)
+
+        def mm(acc, left, cols, right, start, stop):
+            nc.tensor.matmul_mx(out=acc[:], lhsT=mx[left][0][:, cols], lhsT_scale=mx[left][1][:, cols],
+                                rhs=mx[right][0], rhs_scale=mx[right][1][:], start=start, stop=stop)
+
+        def pack_hidden(g, engines):
+            t = packed()
+            ready["h", g] = t
+            for half in range(2):
+                part = slice(2 * half, 2 * half + 2)
+                copy(engines[half], t[:].rearrange("p (t m j) -> p t m j", t=4, j=4)[:, part],
+                     raw["h", g][:].rearrange("p (j m t) -> p t m j", j=4, t=4)[:, part])
+
+        def pack_r(c, r, oh, engine):
+            t = packed()
+            ready["r", c, r, oh] = t
+            src = raw["r", c, r, oh]
+            copy(engine, t[:].rearrange("p (x i u e) -> p x u e i", i=4, u=2, e=2),
+                 src.rearrange("p e u (x i) -> p x u e i", i=4))
+
+        def pack_dh(c, g, engine):
+            t = packed()
+            ready["b", c, g] = t
+            copy(engine, t[:].rearrange("p (x i t) -> p x t i", i=4, t=4),
+                 dh[c, LAB, g][:].rearrange("p (t x i) -> p x t i", t=4, i=4))
+
+        def turn_grad(c, r):
+            t = packed()
+            ready["z", c, r] = t
+            words = raw["z", c, r][:].bitcast(F32)
+            for u in range(2):
+                acc = bank()
+                for w in range(2):
+                    for b in range(2):
+                        first = (2 * b + u) * 256 + w
+                        nc.tensor.transpose(acc[:, (2 * w + b) * P:(2 * w + b + 1) * P],
+                                            words[:, first:first + 255:2], ident[:])
+                nc.vector.tensor_tensor(
+                    out=t[:, u * 1024:(u + 1) * 1024].rearrange("p (n w e) -> p n w e", w=2, e=2),
+                    in0=acc[:].bitcast(BF16).rearrange("p (w n e) -> p n w e", w=2, e=2),
+                    in1=vs[:, c, :].rearrange("p (w e) -> p w e", e=2).unsqueeze(1).to_broadcast([P, 256, 2, 2]),
+                    op=mybir.AluOpType.mult)
+
+        def turn_wk(c, oh, g, engines):
+            t = packed()
+            ready["w", c, oh, g] = t
+            words = raw["w", c, oh][:].bitcast(F32)
+            for pair in range(2):
+                acc = bank()
+                for w in range(2):
+                    for s in range(2):
+                        first = (2 * pair + s) * N + g * 256 + w
+                        nc.tensor.transpose(acc[:, (2 * w + s) * P:(2 * w + s + 1) * P],
+                                            words[:, first:first + 255:2], ident[:])
+                copy(engines[pair], t[:].bitcast(F32)[:, pair * N:(pair + 1) * N].rearrange("p (n w) -> p n w", w=2),
+                     acc[:].rearrange("p (w n) -> p n w", w=2))
+
+        def make_dh(c, r, g, engines):
+            x = ring(sb, "dh", 3, [P, 4 * N], BF16)
+            dh[c, r, g] = x
+            for t in range(4):
+                acc = bank()
+                mm(acc, ("h", g), slice(t * P, (t + 1) * P), ("z", c, r), True, True)
+                copy(engines[t], x[:, t * N:(t + 1) * N], acc[:])
+
+        def turn_dh(c, r, g, engines):
+            t = packed()
+            ready["a", c, r, g] = t
+            words = dh[c, r, g][:].bitcast(F32)
+            for pair in range(2):
+                acc = bank()
+                for tt in range(2):
+                    for u in range(2):
+                        first = (2 * pair + tt) * 256 + u * P
+                        nc.tensor.transpose(acc[:, (2 * tt + u) * P:(2 * tt + u + 1) * P],
+                                            words[:, first:first + P], ident[:])
+                copy(engines[pair], t[:].bitcast(F32).rearrange("p (m a x) -> p m a x", a=2, x=4)[:, :, pair, :],
+                     acc[:].rearrange("p (x m) -> p m x", x=4))
+
+        def grad_emb(c, u, engines):
+            for b in range(2):
+                k = 2 * u + b
+                st = ring(sb, "stage", STAGE, [P, H], F32)
+                for oh in range(2):
+                    acc = bank()
+                    for g in range(2):
+                        mm(acc, ("b", c, g), slice(k * P, (k + 1) * P), ("w", c, oh, g), g == 0, g == 1)
+                    copy(engines[2 * b + oh], st[:, oh * N:(oh + 1) * N], acc[:])
+                nc.sync.dma_start(out=out_0[c].rearrange("(b q u) o -> b u q o", b=2, u=2)[b, u], in_=st[:])
+
+        def grad_wk(c, g, oh, engines):
+            for pair in range(2):
+                st = ring(sb, "stage", STAGE, [P, H], F32)
+                for a in range(2):
+                    k = 2 * pair + a
+                    acc = bank()
+                    for r in (LAB, TOK):
+                        mm(acc, ("r", c, r, oh), slice(k * P, (k + 1) * P), ("a", c, r, g), r == LAB, r == TOK)
+                    copy(engines[k], st[:, a * N:(a + 1) * N], acc[:])
+                first = oh * N + pair * 256
+                nc.sync.dma_start(out=out_1[c, first:first + 256, g * N:(g + 1) * N].rearrange("(a q) h -> q a h", a=2),
+                                  in_=st[:].rearrange("q (a h) -> q a h", a=2))
+
+        q = quantise
+        AAAA, AVAV, AAAV, VAVA = (A, A, A, A), (A, V, A, V), (A, A, A, V), (V, A, V, A)
+        AA, AV, VA, VAAA = (A, A), (A, V), (V, A), (V, A, A, A)
+
+        load_vsum()
+        load_grad(0, LAB)
+        load_hidden(0)
+        load_wk(0, 0)
+        load_hidden(1)
+        load_wk(0, 1)
+        load_grad(0, TOK)
+        load_emb(0)
+        load_query(0, 0)
+        load_grad(1, LAB)
+        load_query(0, 1)
+
+        def pack_r_half(c, oh):
+            pack_r(c, LAB, oh, V)
+            pack_r(c, TOK, oh, V)
+
+        def q_r_half(c, oh):
+            q(("r", c, LAB, oh))
+            q(("r", c, TOK, oh))
+
+        turn_grad(0, LAB)
+        pack_hidden(0, (V, A))
+        q(("z", 0, LAB))
+        q(("h", 0))
+        pack_hidden(1, (V, V))
+        q(("h", 1))
+        make_dh(0, LAB, 0, AAAA)
+        turn_wk(0, 0, 0, AA)
+        turn_wk(0, 0, 1, AA)
+        pack_dh(0, 0, V)
+        q(("w", 0, 0, 0))
+        q(("b", 0, 0))
+        q(("w", 0, 0, 1))
+        make_dh(0, LAB, 1, AAAV)
+        turn_wk(0, 1, 0, AV)
+        turn_wk(0, 1, 1, AA)
+        pack_dh(0, 1, V)
+        turn_grad(0, TOK)
+        load_wk(1, 0)
+        load_wk(1, 1)
+        load_emb(1)
+        load_grad(1, TOK)
+        q(("b", 0, 1))
+        q(("w", 0, 1, 0))
+        q(("w", 0, 1, 1))
+        q(("z", 0, TOK))
+        turn_dh(0, LAB, 0, AA)
+        turn_dh(0, LAB, 1, AA)
+        load_query(1, 0)
+        pack_r_half(0, 0)
+        load_query(1, 1)
+        grad_emb(0, 0, AAAA)
+        make_dh(0, TOK, 0, AAAA)
+        q(("a", 0, LAB, 0))
+        q_r_half(0, 0)
+        q(("a", 0, LAB, 1))
+        grad_emb(0, 1, AAAV)
+        turn_dh(0, TOK, 0, VA)
+        turn_grad(1, LAB)
+        make_dh(0, TOK, 1, AAAA)
+        q(("a", 0, TOK, 0))
+        q(("z", 1, LAB))
+        pack_r_half(0, 1)
+        q_r_half(0, 1)
+        grad_wk(0, 0, 0, AAAA)
+        turn_dh(0, TOK, 1, AA)
+        turn_wk(1, 0, 0, AV)
+        q(("a", 0, TOK, 1))
+        q(("w", 1, 0, 0))
+        make_dh(1, LAB, 0, AAAV)
+        grad_wk(0, 0, 1, VAAA)
+        pack_dh(1, 0, V)
+        turn_wk(1, 0, 1, AA)
+        q(("b", 1, 0))
+        make_dh(1, LAB, 1, (V, A, A, V))
+        q(("w", 1, 0, 1))
+        grad_wk(0, 1, 0, AAAA)
+        pack_dh(1, 1, V)
+        q(("b", 1, 1))
+        turn_wk(1, 1, 0, AV)
+        turn_wk(1, 1, 1, AA)
+        q(("w", 1, 1, 0))
+        q(("w", 1, 1, 1))
+        grad_wk(0, 1, 1, (A, V, A, V))
+        turn_grad(1, TOK)
+        turn_dh(1, LAB, 0, AA)
+        q(("z", 1, TOK))
+        pack_r_half(1, 0)
+        grad_emb(1, 0, AAAA)
+        make_dh(1, TOK, 0, AAAA)
+        q(("a", 1, LAB, 0))
+        q_r_half(1, 0)
+        turn_dh(1, LAB, 1, (V, V))
+        turn_dh(1, TOK, 0, AA)
+        grad_emb(1, 1, AAAA)
+        q(("a", 1, TOK, 0))
+        q(("a", 1, LAB, 1))
+        make_dh(1, TOK, 1, AAAA)
+        pack_r_half(1, 1)
+        q_r_half(1, 1)
+        grad_wk(1, 0, 0, AAAV)
+        turn_dh(1, TOK, 1, VA)
+        q(("a", 1, TOK, 1))
+        grad_wk(1, 0, 1, AAAA)
+        grad_wk(1, 1, 0, VAVA)
+        grad_wk(1, 1, 1, VAVA)

@@ -17,7 +17,8 @@ E5M2 = mybir.dt.float8_e5m2_x4
 P = 128
 N = 512
 TOK, LAB = 0, 1
-STAGE = 12
+STAGE = 6
+DH = 4
 
 
 def tile_relationtagger_pa_v_kernel(tc, hidden, emb, Wk, Wq, vsum, query, grad_out, out_0, out_1):
@@ -65,11 +66,13 @@ def tile_relationtagger_pa_v_kernel(tc, hidden, emb, Wk, Wq, vsum, query, grad_o
             nc.sync.dma_start(out=t[:].rearrange("p (t h) -> p t h", t=4),
                               in_=hidden[0, :, g * N:(g + 1) * N].rearrange("(p t) h -> p t h", t=4))
 
-        def load_grad(c, r):
+        def load_grad(c, r, pieces=1):
             t = ring(sb, "raw_g", 3, [P, 4 * N], BF16)
             raw["z", c, r] = t
-            nc.sync.dma_start(out=t[:].rearrange("q (b x) -> q b x", b=2),
-                              in_=grad_out[0, c, r * N:(r + 1) * N, :].rearrange("(b q u) j -> q b (u j)", b=2, u=2))
+            rows = grad_out[0, c, r * N:(r + 1) * N, :].rearrange("(q s) j -> q (s j)", s=4)
+            width = 4 * N // pieces
+            for k in range(pieces):
+                nc.sync.dma_start(out=t[:, k * width:(k + 1) * width], in_=rows[:, k * width:(k + 1) * width])
 
         def load_wk(c, oh):
             t = ring(sb, "raw_w", 2, [P, 4 * H], BF16)
@@ -81,22 +84,23 @@ def tile_relationtagger_pa_v_kernel(tc, hidden, emb, Wk, Wq, vsum, query, grad_o
             t = ring(sb, "raw_e", 2, [P, 4 * H], BF16)
             nc.sync.dma_start(out=t[:], in_=emb[c].rearrange("(p j) o -> p (j o)", j=4))
             for oh in range(2):
-                raw["r", c, LAB, oh] = t[:].rearrange("p (e u o) -> p e u o", e=2, u=2)[:, :, :, oh * N:(oh + 1) * N]
+                raw["r", c, LAB, oh] = t[:].rearrange("p (j o) -> p j o", j=4)[:, :, oh * N:(oh + 1) * N]
 
         def load_query(c, oh):
             t = ring(sb, "raw_q", 3, [P, 4 * N], F32)
             nc.sync.dma_start(out=t[:].rearrange("p (j o) -> p j o", j=4),
                               in_=query[c, 0, :, oh * N:(oh + 1) * N].rearrange("(p j) o -> p j o", j=4))
-            raw["r", c, TOK, oh] = t[:].rearrange("p (e u o) -> p e u o", e=2, u=2)
+            raw["r", c, TOK, oh] = t[:].rearrange("p (j o) -> p j o", j=4)
 
-        def quantise(key):
+        def quantise(key, parts=(0, 1)):
             kind = key[0]
-            depth = {"h": 2, "z": 3, "w": 4, "r": 8, "a": 6, "b": 2}[kind]
-            codes = ring(sb, "codes_" + kind, depth, [P, N], U32)
-            scales = ring(sb, "scales_" + kind, depth, [P, N], U8)
-            view = codes[:].bitcast(E5M2 if kind in "zab" else E4M3)
-            nc.vector.quantize_mx(out=view, scales=scales[:], in_=ready[key][:])
-            mx[key] = (view, scales)
+            if key not in mx:
+                depth = {"h": 2, "z": 3, "w": 4, "r": 8, "a": 6, "b": 2}[kind]
+                codes = ring(sb, "codes_" + kind, depth, [P, N], U32)
+                scales = ring(sb, "scales_" + kind, depth, [P, N], U8)
+                mx[key] = (codes[:].bitcast(E5M2 if kind in "zab" else E4M3), scales)
+            lo, hi = parts[0] * 256, (parts[-1] + 1) * 256
+            nc.vector.quantize_mx(out=mx[key][0][:, lo:hi], scales=mx[key][1][:, lo:hi], in_=ready[key][:, 4 * lo:4 * hi])
 
         def mm(acc, left, cols, right, start, stop):
             nc.tensor.matmul_mx(out=acc[:], lhsT=mx[left][0][:, cols], lhsT_scale=mx[left][1][:, cols],
@@ -105,37 +109,35 @@ def tile_relationtagger_pa_v_kernel(tc, hidden, emb, Wk, Wq, vsum, query, grad_o
         def pack_hidden(g, engines):
             t = packed()
             ready["h", g] = t
-            for half in range(2):
-                part = slice(2 * half, 2 * half + 2)
-                copy(engines[half], t[:].rearrange("p (t m j) -> p t m j", t=4, j=4)[:, part],
-                     raw["h", g][:].rearrange("p (j m t) -> p t m j", j=4, t=4)[:, part])
+            for u in range(2):
+                copy(engines[u], t[:].rearrange("p (u m e j) -> p u m j e", u=2, e=2, j=4)[:, u],
+                     raw["h", g][:].rearrange("p (j m u e) -> p u m j e", j=4, u=2, e=2)[:, u])
+
+        def pack(key, src, engine):
+            t = packed()
+            ready[key] = t
+            copy(engine, t[:].rearrange("p (x i j) -> p x j i", i=4, j=4), src.rearrange("p j (x i) -> p x j i", i=4))
 
         def pack_r(c, r, oh, engine):
-            t = packed()
-            ready["r", c, r, oh] = t
-            src = raw["r", c, r, oh]
-            copy(engine, t[:].rearrange("p (x i u e) -> p x u e i", i=4, u=2, e=2),
-                 src.rearrange("p e u (x i) -> p x u e i", i=4))
+            pack(("r", c, r, oh), raw["r", c, r, oh], engine)
 
-        def pack_dh(c, g, engine):
-            t = packed()
-            ready["b", c, g] = t
-            copy(engine, t[:].rearrange("p (x i t) -> p x t i", i=4, t=4),
-                 dh[c, LAB, g][:].rearrange("p (t x i) -> p x t i", t=4, i=4))
+        def pack_dh(c, r, g, engine):
+            pack(("a", c, r, g), dh[c, r, g][:].rearrange("p (j n) -> p j n", j=4), engine)
 
-        def turn_grad(c, r):
-            t = packed()
-            ready["z", c, r] = t
+        def turn_grad(c, r, pairs=(0, 1)):
+            if ("z", c, r) not in ready:
+                ready["z", c, r] = packed()
+            t = ready["z", c, r]
             words = raw["z", c, r][:].bitcast(F32)
-            for u in range(2):
+            for pair in pairs:
                 acc = bank()
                 for w in range(2):
-                    for b in range(2):
-                        first = (2 * b + u) * 256 + w
-                        nc.tensor.transpose(acc[:, (2 * w + b) * P:(2 * w + b + 1) * P],
+                    for s in range(2):
+                        first = (2 * pair + s) * 256 + w
+                        nc.tensor.transpose(acc[:, (2 * w + s) * P:(2 * w + s + 1) * P],
                                             words[:, first:first + 255:2], ident[:])
                 nc.vector.tensor_tensor(
-                    out=t[:, u * 1024:(u + 1) * 1024].rearrange("p (n w e) -> p n w e", w=2, e=2),
+                    out=t[:, pair * 1024:(pair + 1) * 1024].rearrange("p (n w e) -> p n w e", w=2, e=2),
                     in0=acc[:].bitcast(BF16).rearrange("p (w n e) -> p n w e", w=2, e=2),
                     in1=vs[:, c, :].rearrange("p (w e) -> p w e", e=2).unsqueeze(1).to_broadcast([P, 256, 2, 2]),
                     op=mybir.AluOpType.mult)
@@ -154,159 +156,164 @@ def tile_relationtagger_pa_v_kernel(tc, hidden, emb, Wk, Wq, vsum, query, grad_o
                 copy(engines[pair], t[:].bitcast(F32)[:, pair * N:(pair + 1) * N].rearrange("p (n w) -> p n w", w=2),
                      acc[:].rearrange("p (w n) -> p n w", w=2))
 
-        def make_dh(c, r, g, engines):
-            x = ring(sb, "dh", 3, [P, 4 * N], BF16)
-            dh[c, r, g] = x
-            for t in range(4):
+        def make_dh(c, r, g, engines, tiles=(0, 1, 2, 3)):
+            if (c, r, g) not in dh:
+                dh[c, r, g] = ring(sb, "dh", DH, [P, 4 * N], BF16)
+            for s in tiles:
                 acc = bank()
-                mm(acc, ("h", g), slice(t * P, (t + 1) * P), ("z", c, r), True, True)
-                copy(engines[t], x[:, t * N:(t + 1) * N], acc[:])
+                mm(acc, ("z", c, r), slice(s * P, (s + 1) * P), ("h", g), True, True)
+                copy(engines[s], dh[c, r, g][:, s * N:(s + 1) * N], acc[:])
 
-        def turn_dh(c, r, g, engines):
+        def turn_dh(c, g, engines):
             t = packed()
-            ready["a", c, r, g] = t
-            words = dh[c, r, g][:].bitcast(F32)
+            ready["b", c, g] = t
+            words = dh[c, LAB, g][:].bitcast(F32)
             for pair in range(2):
                 acc = bank()
-                for tt in range(2):
-                    for u in range(2):
-                        first = (2 * pair + tt) * 256 + u * P
-                        nc.tensor.transpose(acc[:, (2 * tt + u) * P:(2 * tt + u + 1) * P],
+                for u in range(2):
+                    for s in range(2):
+                        first = (2 * pair + s) * 256 + u * P
+                        nc.tensor.transpose(acc[:, (2 * u + s) * P:(2 * u + s + 1) * P],
                                             words[:, first:first + P], ident[:])
-                copy(engines[pair], t[:].bitcast(F32).rearrange("p (m a x) -> p m a x", a=2, x=4)[:, :, pair, :],
-                     acc[:].rearrange("p (x m) -> p m x", x=4))
+                copy(engines[pair], t[:].bitcast(F32)[:, pair * N:(pair + 1) * N].rearrange("p (n w) -> p n w", w=2),
+                     acc[:].rearrange("p (w n) -> p n w", w=2))
 
-        def grad_emb(c, u, engines):
-            for b in range(2):
-                k = 2 * u + b
-                st = ring(sb, "stage", STAGE, [P, H], F32)
+        def grad_emb(c, pair, engines):
+            st = ring(sb, "stage", STAGE, [P, 2 * H], F32)
+            for a in range(2):
+                s = 2 * pair + a
                 for oh in range(2):
                     acc = bank()
                     for g in range(2):
-                        mm(acc, ("b", c, g), slice(k * P, (k + 1) * P), ("w", c, oh, g), g == 0, g == 1)
-                    copy(engines[2 * b + oh], st[:, oh * N:(oh + 1) * N], acc[:])
-                nc.sync.dma_start(out=out_0[c].rearrange("(b q u) o -> b u q o", b=2, u=2)[b, u], in_=st[:])
+                        mm(acc, ("b", c, g), slice(s * P, (s + 1) * P), ("w", c, oh, g), g == 0, g == 1)
+                    copy(engines[2 * a + oh], st[:, a * H + oh * N:a * H + (oh + 1) * N], acc[:])
+                nc.sync.dma_start(out=out_0[c].rearrange("(q s) o -> s q o", s=4)[s], in_=st[:, a * H:(a + 1) * H])
 
-        def grad_wk(c, g, oh, engines):
-            for pair in range(2):
-                st = ring(sb, "stage", STAGE, [P, H], F32)
-                for a in range(2):
-                    k = 2 * pair + a
+        def grad_wk(c, oh, pair, engines):
+            st = ring(sb, "stage", STAGE, [P, 2 * H], F32)
+            for a in range(2):
+                k = 2 * pair + a
+                for g in range(2):
                     acc = bank()
                     for r in (LAB, TOK):
                         mm(acc, ("r", c, r, oh), slice(k * P, (k + 1) * P), ("a", c, r, g), r == LAB, r == TOK)
-                    copy(engines[k], st[:, a * N:(a + 1) * N], acc[:])
-                first = oh * N + pair * 256
-                nc.sync.dma_start(out=out_1[c, first:first + 256, g * N:(g + 1) * N].rearrange("(a q) h -> q a h", a=2),
-                                  in_=st[:].rearrange("q (a h) -> q a h", a=2))
+                    cols = st[:, a * H + g * N:a * H + (g + 1) * N]
+                    copy(engines[2 * a + g], cols.rearrange("p (m u e) -> p m u e", u=2, e=2),
+                         acc[:].rearrange("p (u m e) -> p m u e", u=2, e=2))
+                first = oh * N + k * P
+                nc.sync.dma_start(out=out_1[c, first:first + P, :], in_=st[:, a * H:(a + 1) * H])
 
         q = quantise
         AAAA, AVAV, AAAV, VAVA = (A, A, A, A), (A, V, A, V), (A, A, A, V), (V, A, V, A)
         AA, AV, VA, VAAA = (A, A), (A, V), (V, A), (V, A, A, A)
 
         load_vsum()
-        load_grad(0, LAB)
         load_hidden(0)
-        load_wk(0, 0)
+        load_grad(0, LAB, 2)
         load_hidden(1)
-        load_wk(0, 1)
         load_grad(0, TOK)
+        load_wk(0, 0)
+        load_wk(0, 1)
         load_emb(0)
         load_query(0, 0)
         load_grad(1, LAB)
         load_query(0, 1)
 
-        def pack_r_half(c, oh):
-            pack_r(c, LAB, oh, V)
-            pack_r(c, TOK, oh, V)
-
-        def q_r_half(c, oh):
-            q(("r", c, LAB, oh))
-            q(("r", c, TOK, oh))
-
-        turn_grad(0, LAB)
         pack_hidden(0, (V, A))
-        q(("z", 0, LAB))
         q(("h", 0))
-        pack_hidden(1, (V, V))
+        turn_grad(0, LAB, (0,))
+        q(("z", 0, LAB), (0,))
+        turn_grad(0, LAB, (1,))
+        q(("z", 0, LAB), (1,))
+        pack_hidden(1, (V, A))
         q(("h", 1))
-        make_dh(0, LAB, 0, AAAA)
-        turn_wk(0, 0, 0, AA)
-        turn_wk(0, 0, 1, AA)
-        pack_dh(0, 0, V)
-        q(("w", 0, 0, 0))
-        q(("b", 0, 0))
-        q(("w", 0, 0, 1))
-        make_dh(0, LAB, 1, AAAV)
-        turn_wk(0, 1, 0, AV)
-        turn_wk(0, 1, 1, AA)
-        pack_dh(0, 1, V)
+        make_dh(0, LAB, 0, (A, A, V, A))
         turn_grad(0, TOK)
+        make_dh(0, LAB, 1, AAAA)
+        q(("z", 0, TOK))
+        pack_dh(0, LAB, 0, V)
+        turn_dh(0, 0, AA)
+        turn_wk(0, 0, 0, AA)
+        make_dh(0, TOK, 0, AAAA, (0, 1))
+        q(("a", 0, LAB, 0))
+        pack_dh(0, LAB, 1, V)
+        q(("b", 0, 0))
+        q(("w", 0, 0, 0))
+        q(("a", 0, LAB, 1))
+        turn_wk(0, 0, 1, AV)
+        make_dh(0, TOK, 0, AAAA, (2, 3))
+        turn_dh(0, 1, AA)
+        turn_wk(0, 1, 0, AA)
+        q(("w", 0, 0, 1))
+        pack_dh(0, TOK, 0, V)
+        q(("b", 0, 1))
+        make_dh(0, TOK, 1, AVAV, (0, 1))
+        turn_wk(0, 1, 1, AA)
+        q(("w", 0, 1, 0))
+        make_dh(0, TOK, 1, AAAA, (2, 3))
         load_wk(1, 0)
         load_wk(1, 1)
         load_emb(1)
         load_grad(1, TOK)
-        q(("b", 0, 1))
-        q(("w", 0, 1, 0))
-        q(("w", 0, 1, 1))
-        q(("z", 0, TOK))
-        turn_dh(0, LAB, 0, AA)
-        turn_dh(0, LAB, 1, AA)
         load_query(1, 0)
-        pack_r_half(0, 0)
-        load_query(1, 1)
-        grad_emb(0, 0, AAAA)
-        make_dh(0, TOK, 0, AAAA)
-        q(("a", 0, LAB, 0))
-        q_r_half(0, 0)
-        q(("a", 0, LAB, 1))
-        grad_emb(0, 1, AAAV)
-        turn_dh(0, TOK, 0, VA)
+        pack_r(0, LAB, 0, V)
+        q(("w", 0, 1, 1))
         turn_grad(1, LAB)
-        make_dh(0, TOK, 1, AAAA)
         q(("a", 0, TOK, 0))
         q(("z", 1, LAB))
-        pack_r_half(0, 1)
-        q_r_half(0, 1)
-        grad_wk(0, 0, 0, AAAA)
-        turn_dh(0, TOK, 1, AA)
-        turn_wk(1, 0, 0, AV)
+        pack_r(0, TOK, 0, V)
+        load_query(1, 1)
+        grad_emb(0, 0, AAAA)
+        pack_dh(0, TOK, 1, V)
+        q(("r", 0, LAB, 0))
+        q(("r", 0, TOK, 0))
         q(("a", 0, TOK, 1))
-        q(("w", 1, 0, 0))
-        make_dh(1, LAB, 0, AAAV)
-        grad_wk(0, 0, 1, VAAA)
-        pack_dh(1, 0, V)
+        turn_wk(1, 0, 0, AA)
+        grad_emb(0, 1, AAAA)
+        make_dh(1, LAB, 0, AAAA)
+        pack_r(0, LAB, 1, V)
+        pack_r(0, TOK, 1, V)
+        q(("r", 0, LAB, 1))
+        q(("r", 0, TOK, 1))
         turn_wk(1, 0, 1, AA)
-        q(("b", 1, 0))
-        make_dh(1, LAB, 1, (V, A, A, V))
+        grad_wk(0, 0, 0, AAAA)
+        make_dh(1, LAB, 1, AAAA)
+        q(("w", 1, 0, 0))
+        pack_dh(1, LAB, 0, V)
         q(("w", 1, 0, 1))
-        grad_wk(0, 1, 0, AAAA)
-        pack_dh(1, 1, V)
-        q(("b", 1, 1))
-        turn_wk(1, 1, 0, AV)
-        turn_wk(1, 1, 1, AA)
-        q(("w", 1, 1, 0))
-        q(("w", 1, 1, 1))
-        grad_wk(0, 1, 1, (A, V, A, V))
+        turn_dh(1, 0, AA)
         turn_grad(1, TOK)
-        turn_dh(1, LAB, 0, AA)
-        q(("z", 1, TOK))
-        pack_r_half(1, 0)
-        grad_emb(1, 0, AAAA)
-        make_dh(1, TOK, 0, AAAA)
         q(("a", 1, LAB, 0))
-        q_r_half(1, 0)
-        turn_dh(1, LAB, 1, (V, V))
-        turn_dh(1, TOK, 0, AA)
-        grad_emb(1, 1, AAAA)
-        q(("a", 1, TOK, 0))
+        grad_wk(0, 0, 1, AAAA)
+        q(("z", 1, TOK))
+        pack_dh(1, LAB, 1, V)
+        q(("b", 1, 0))
         q(("a", 1, LAB, 1))
+        turn_dh(1, 1, AA)
+        turn_wk(1, 1, 0, AV)
+        grad_wk(0, 1, 0, AAAA)
+        q(("b", 1, 1))
+        q(("w", 1, 1, 0))
+        pack_r(1, LAB, 0, V)
+        make_dh(1, TOK, 0, (A, A, V, V))
+        turn_wk(1, 1, 1, AV)
+        grad_wk(0, 1, 1, AAAA)
+        q(("w", 1, 1, 1))
+        pack_dh(1, TOK, 0, V)
         make_dh(1, TOK, 1, AAAA)
-        pack_r_half(1, 1)
-        q_r_half(1, 1)
-        grad_wk(1, 0, 0, AAAV)
-        turn_dh(1, TOK, 1, VA)
+        pack_r(1, TOK, 0, V)
+        q(("r", 1, LAB, 0))
+        q(("a", 1, TOK, 0))
+        q(("r", 1, TOK, 0))
+        pack_dh(1, TOK, 1, V)
+        grad_emb(1, 0, AAAA)
         q(("a", 1, TOK, 1))
-        grad_wk(1, 0, 1, AAAA)
+        grad_emb(1, 1, AAAA)
+        pack_r(1, LAB, 1, V)
+        pack_r(1, TOK, 1, V)
+        q(("r", 1, LAB, 1))
+        q(("r", 1, TOK, 1))
+        grad_wk(1, 0, 0, AAAA)
+        grad_wk(1, 0, 1, (A, A, V, V))
         grad_wk(1, 1, 0, VAVA)
         grad_wk(1, 1, 1, VAVA)

@@ -16,9 +16,20 @@ E5M2 = mybir.dt.float8_e5m2_x4
 
 P = 128
 N = 512
+HALF = N // 2
 TOK, LAB = 0, 1
-STAGE = 6
-DH = 4
+WHOLE = (0, 1)
+
+BANKS = 8
+PACKED = 8
+DH_TILES = 4
+STAGES = 12
+RAW_DEPTH = {"half_mb": 4, "wk": 2, "emb": 2, "query": 3}
+CODE_DEPTH = {"hidden": 2, "dz": 3, "wk": 4, "r": 8, "dh_rows": 8, "dh_feat": 2}
+FORMAT = {"hidden": E4M3, "wk": E4M3, "r": E4M3, "dz": E5M2, "dh_rows": E5M2, "dh_feat": E5M2}
+
+BY_ROWS = ((0, 0), (0, 1), (1, 0), (1, 1))
+BY_HALVES = ((0, 0), (1, 0), (0, 1), (1, 1))
 
 
 def tile_relationtagger_pa_v_kernel(tc, hidden, emb, Wk, Wq, vsum, query, grad_out, out_0, out_1):
@@ -29,291 +40,296 @@ def tile_relationtagger_pa_v_kernel(tc, hidden, emb, Wk, Wq, vsum, query, grad_o
         ctx.enter_context(tc.manual_schedule())
 
         taken = {}
+        raw, packed, mx, dh = {}, {}, {}, {}
+        free_slots = list(range(PACKED))
+        slot_of = {}
 
-        def ring(pool, kind, depth, shape, dtype):
-            k = taken.get(kind, 0)
-            taken[kind] = k + 1
-            slot = "%s%d" % (kind, k % depth)
-            if pool is ps:
-                return pool.tile(shape, dtype, name=slot, tag=slot)
-            return pool.tile(shape, dtype, name=slot, tag=slot, align_bytes=64)
+        def ring(kind, depth, shape, dtype):
+            count = taken.get(kind, 0)
+            taken[kind] = count + 1
+            slot = "%s%d" % (kind, count % depth)
+            return sb.tile(shape, dtype, name=slot, tag=slot, align_bytes=64)
 
         def bank():
-            return ring(ps, "bank", 8, [P, N], F32)
+            count = taken.get("bank", 0)
+            taken["bank"] = count + 1
+            slot = "bank%d" % (count % BANKS)
+            return ps.tile([P, N], F32, name=slot, tag=slot)
 
-        def packed():
-            return ring(sb, "packed", 8, [P, 4 * N], BF16)
+        def packed_tile(key):
+            if key not in packed:
+                slot_of[key] = free_slots.pop(0)
+                slot = "packed%d" % slot_of[key]
+                packed[key] = sb.tile([P, 4 * N], BF16, name=slot, tag=slot, align_bytes=64)
+            return packed[key]
 
-        def copy(engine, out, in_):
-            if engine is nc.scalar:
-                engine.copy(out=out, in_=in_)
+        def empty_bank(on_vector, out, in_):
+            if on_vector:
+                nc.vector.tensor_copy(out=out, in_=in_)
             else:
-                engine.tensor_copy(out=out, in_=in_)
-
-        V, A = nc.vector, nc.scalar
-        raw, ready, mx, dh, staged = {}, {}, {}, {}, {}
+                nc.scalar.copy(out=out, in_=in_)
 
         ident = sb.tile([P, P], F32, name="ident", align_bytes=64)
         make_identity(nc, ident[:])
         vs = sb.tile([P, C, 4], BF16, name="vs", align_bytes=64)
 
+
         def load_vsum():
             nc.scalar.dma_start(out=vs[:], in_=vsum[:, 0, :].rearrange("c (p t) -> p c t", t=4))
 
         def load_hidden(g):
-            t = ring(sb, "raw_h", 2, [P, 4 * N], BF16)
-            raw["h", g] = t
+            t = ring("raw_half_mb", RAW_DEPTH["half_mb"], [P, 4 * N], BF16)
+            raw["hidden", g] = t
             nc.sync.dma_start(out=t[:].rearrange("p (t h) -> p t h", t=4),
                               in_=hidden[0, :, g * N:(g + 1) * N].rearrange("(p t) h -> p t h", t=4))
 
         def load_grad(c, r, pieces=1):
-            t = ring(sb, "raw_g", 3, [P, 4 * N], BF16)
-            raw["z", c, r] = t
+            t = ring("raw_half_mb", RAW_DEPTH["half_mb"], [P, 4 * N], BF16)
+            raw["dz", c, r] = t
             rows = grad_out[0, c, r * N:(r + 1) * N, :].rearrange("(q s) j -> q (s j)", s=4)
             width = 4 * N // pieces
             for k in range(pieces):
                 nc.sync.dma_start(out=t[:, k * width:(k + 1) * width], in_=rows[:, k * width:(k + 1) * width])
 
         def load_wk(c, oh):
-            t = ring(sb, "raw_w", 2, [P, 4 * H], BF16)
-            raw["w", c, oh] = t
+            t = ring("raw_wk", RAW_DEPTH["wk"], [P, 4 * H], BF16)
+            raw["wk", c, oh] = t
             nc.sync.dma_start(out=t[:].rearrange("m (s h) -> m s h", s=4),
                               in_=Wk[c, oh * N:(oh + 1) * N, :].rearrange("(s m) h -> m s h", s=4))
 
         def load_emb(c):
-            t = ring(sb, "raw_e", 2, [P, 4 * H], BF16)
-            nc.sync.dma_start(out=t[:], in_=emb[c].rearrange("(p j) o -> p (j o)", j=4))
+            t = ring("raw_emb", RAW_DEPTH["emb"], [P, 4 * H], BF16)
+            nc.sync.dma_start(out=t[:], in_=emb[c].rearrange("(p t) o -> p (t o)", t=4))
             for oh in range(2):
-                raw["r", c, LAB, oh] = t[:].rearrange("p (j o) -> p j o", j=4)[:, :, oh * N:(oh + 1) * N]
+                raw["r", c, LAB, oh] = t[:].rearrange("p (t o) -> p t o", t=4)[:, :, oh * N:(oh + 1) * N]
 
         def load_query(c, oh):
-            t = ring(sb, "raw_q", 3, [P, 4 * N], F32)
-            nc.sync.dma_start(out=t[:].rearrange("p (j o) -> p j o", j=4),
-                              in_=query[c, 0, :, oh * N:(oh + 1) * N].rearrange("(p j) o -> p j o", j=4))
-            raw["r", c, TOK, oh] = t[:].rearrange("p (j o) -> p j o", j=4)
+            t = ring("raw_query", RAW_DEPTH["query"], [P, 4 * N], F32)
+            nc.sync.dma_start(out=t[:].rearrange("p (t o) -> p t o", t=4),
+                              in_=query[c, 0, :, oh * N:(oh + 1) * N].rearrange("(p t) o -> p t o", t=4))
+            raw["r", c, TOK, oh] = t[:].rearrange("p (t o) -> p t o", t=4)
 
-        def quantise(key, parts=(0, 1)):
+
+        def pack_hidden(g):
+            dst = packed_tile(("hidden", g))[:].rearrange("p (u m e t) -> p u m t e", u=2, e=2, t=4)
+            src = raw["hidden", g][:].rearrange("p (t m u e) -> p u m t e", t=4, u=2, e=2)
+            nc.vector.tensor_copy(out=dst[:, 0], in_=src[:, 0])
+            nc.scalar.copy(out=dst[:, 1], in_=src[:, 1])
+
+        def pack(key, src, halves):
+            lo, hi = halves[0] * HALF, (halves[-1] + 1) * HALF
+            nc.vector.tensor_copy(
+                out=packed_tile(key)[:, 4 * lo:4 * hi].rearrange("p (x i t) -> p x t i", i=4, t=4),
+                in_=src[:, :, lo:hi].rearrange("p t (x i) -> p x t i", i=4))
+
+        def pack_r(c, r, oh, halves=WHOLE):
+            pack(("r", c, r, oh), raw["r", c, r, oh], halves)
+
+        def pack_dh(c, r, g):
+            pack(("dh_rows", c, r, g), dh[c, r, g][:].rearrange("p (t n) -> p t n", t=4), WHOLE)
+
+
+        def turn(pairs, starts, step):
+            acc = bank()
+            for w in range(2):
+                for s in range(2):
+                    first = starts[w][s]
+                    nc.tensor.transpose(acc[:, (2 * w + s) * P:(2 * w + s + 1) * P],
+                                        pairs[:, first:first + (P - 1) * step + 1:step], ident[:])
+            return acc
+
+        def empty_turned(on_vector, key, half, acc):
+            dst = packed_tile(key)[:].bitcast(F32)[:, half * N:(half + 1) * N]
+            empty_bank(on_vector, dst.rearrange("p (n w) -> p n w", w=2), acc[:].rearrange("p (w n) -> p n w", w=2))
+
+        def turn_grad(c, r, halves=WHOLE):
+            t = packed_tile(("dz", c, r))
+            pairs = raw["dz", c, r][:].bitcast(F32)
+            for half in halves:
+                acc = turn(pairs, [[(2 * half + s) * HALF + w for s in range(2)] for w in range(2)], 2)
+                nc.vector.tensor_tensor(
+                    out=t[:, half * 4 * HALF:(half + 1) * 4 * HALF].rearrange("p (n w e) -> p n w e", w=2, e=2),
+                    in0=acc[:].bitcast(BF16).rearrange("p (w n e) -> p n w e", w=2, e=2),
+                    in1=vs[:, c, :].rearrange("p (w e) -> p w e", e=2).unsqueeze(1).to_broadcast([P, HALF, 2, 2]),
+                    op=mybir.AluOpType.mult)
+
+        def turn_wk(c, oh, g, vector=()):
+            packed_tile(("wk", c, oh, g))
+            pairs = raw["wk", c, oh][:].bitcast(F32)
+            for half in WHOLE:
+                acc = turn(pairs, [[(2 * half + s) * N + g * HALF + w for s in range(2)] for w in range(2)], 2)
+                empty_turned(half in vector, ("wk", c, oh, g), half, acc)
+
+        def turn_dh(c, g, vector=()):
+            packed_tile(("dh_feat", c, g))
+            pairs = dh[c, LAB, g][:].bitcast(F32)
+            for half in WHOLE:
+                acc = turn(pairs, [[(2 * half + s) * HALF + w * P for s in range(2)] for w in range(2)], 1)
+                empty_turned(half in vector, ("dh_feat", c, g), half, acc)
+
+
+        def quantise(*key, halves=WHOLE):
             kind = key[0]
             if key not in mx:
-                depth = {"h": 2, "z": 3, "w": 4, "r": 8, "a": 6, "b": 2}[kind]
-                codes = ring(sb, "codes_" + kind, depth, [P, N], U32)
-                scales = ring(sb, "scales_" + kind, depth, [P, N], U8)
-                mx[key] = (codes[:].bitcast(E5M2 if kind in "zab" else E4M3), scales)
-            lo, hi = parts[0] * 256, (parts[-1] + 1) * 256
-            nc.vector.quantize_mx(out=mx[key][0][:, lo:hi], scales=mx[key][1][:, lo:hi], in_=ready[key][:, 4 * lo:4 * hi])
+                codes = ring("codes_" + kind, CODE_DEPTH[kind], [P, N], U32)
+                scales = ring("scales_" + kind, CODE_DEPTH[kind], [P, N], U8)
+                mx[key] = (codes[:].bitcast(FORMAT[kind]), scales)
+            lo, hi = halves[0] * HALF, (halves[-1] + 1) * HALF
+            nc.vector.quantize_mx(out=mx[key][0][:, lo:hi], scales=mx[key][1][:, lo:hi],
+                                  in_=packed[key][:, 4 * lo:4 * hi])
+            if halves[-1] == WHOLE[-1]:
+                free_slots.append(slot_of[key])
 
-        def mm(acc, left, cols, right, start, stop):
+        def mm(acc, left, part, right, start, stop):
+            cols = slice(part * P, (part + 1) * P)
             nc.tensor.matmul_mx(out=acc[:], lhsT=mx[left][0][:, cols], lhsT_scale=mx[left][1][:, cols],
                                 rhs=mx[right][0], rhs_scale=mx[right][1][:], start=start, stop=stop)
 
-        def pack_hidden(g, engines):
-            t = packed()
-            ready["h", g] = t
-            for u in range(2):
-                copy(engines[u], t[:].rearrange("p (u m e j) -> p u m j e", u=2, e=2, j=4)[:, u],
-                     raw["h", g][:].rearrange("p (j m u e) -> p u m j e", j=4, u=2, e=2)[:, u])
-
-        def pack(key, src, engine):
-            t = packed()
-            ready[key] = t
-            copy(engine, t[:].rearrange("p (x i j) -> p x j i", i=4, j=4), src.rearrange("p j (x i) -> p x j i", i=4))
-
-        def pack_r(c, r, oh, engine):
-            pack(("r", c, r, oh), raw["r", c, r, oh], engine)
-
-        def pack_dh(c, r, g, engine):
-            pack(("a", c, r, g), dh[c, r, g][:].rearrange("p (j n) -> p j n", j=4), engine)
-
-        def turn_grad(c, r, pairs=(0, 1)):
-            if ("z", c, r) not in ready:
-                ready["z", c, r] = packed()
-            t = ready["z", c, r]
-            words = raw["z", c, r][:].bitcast(F32)
-            for pair in pairs:
-                acc = bank()
-                for w in range(2):
-                    for s in range(2):
-                        first = (2 * pair + s) * 256 + w
-                        nc.tensor.transpose(acc[:, (2 * w + s) * P:(2 * w + s + 1) * P],
-                                            words[:, first:first + 255:2], ident[:])
-                nc.vector.tensor_tensor(
-                    out=t[:, pair * 1024:(pair + 1) * 1024].rearrange("p (n w e) -> p n w e", w=2, e=2),
-                    in0=acc[:].bitcast(BF16).rearrange("p (w n e) -> p n w e", w=2, e=2),
-                    in1=vs[:, c, :].rearrange("p (w e) -> p w e", e=2).unsqueeze(1).to_broadcast([P, 256, 2, 2]),
-                    op=mybir.AluOpType.mult)
-
-        def turn_wk(c, oh, g, engines):
-            t = packed()
-            ready["w", c, oh, g] = t
-            words = raw["w", c, oh][:].bitcast(F32)
-            for pair in range(2):
-                acc = bank()
-                for w in range(2):
-                    for s in range(2):
-                        first = (2 * pair + s) * N + g * 256 + w
-                        nc.tensor.transpose(acc[:, (2 * w + s) * P:(2 * w + s + 1) * P],
-                                            words[:, first:first + 255:2], ident[:])
-                copy(engines[pair], t[:].bitcast(F32)[:, pair * N:(pair + 1) * N].rearrange("p (n w) -> p n w", w=2),
-                     acc[:].rearrange("p (w n) -> p n w", w=2))
-
-        def make_dh(c, r, g, engines, tiles=(0, 1, 2, 3)):
+        def make_dh(c, r, g, slices=(0, 1, 2, 3), vector=()):
             if (c, r, g) not in dh:
-                dh[c, r, g] = ring(sb, "dh", DH, [P, 4 * N], BF16)
-            for s in tiles:
+                dh[c, r, g] = ring("dh", DH_TILES, [P, 4 * N], BF16)
+            for s in slices:
                 acc = bank()
-                mm(acc, ("z", c, r), slice(s * P, (s + 1) * P), ("h", g), True, True)
-                copy(engines[s], dh[c, r, g][:, s * N:(s + 1) * N], acc[:])
+                mm(acc, ("dz", c, r), s, ("hidden", g), True, True)
+                empty_bank(s in vector, dh[c, r, g][:, s * N:(s + 1) * N], acc[:])
 
-        def turn_dh(c, g, engines):
-            t = packed()
-            ready["b", c, g] = t
-            words = dh[c, LAB, g][:].bitcast(F32)
-            for pair in range(2):
-                acc = bank()
-                for u in range(2):
-                    for s in range(2):
-                        first = (2 * pair + s) * 256 + u * P
-                        nc.tensor.transpose(acc[:, (2 * u + s) * P:(2 * u + s + 1) * P],
-                                            words[:, first:first + P], ident[:])
-                copy(engines[pair], t[:].bitcast(F32)[:, pair * N:(pair + 1) * N].rearrange("p (n w) -> p n w", w=2),
-                     acc[:].rearrange("p (w n) -> p n w", w=2))
-
-        def grad_emb(c, pair, engines):
-            st = ring(sb, "stage", STAGE, [P, 2 * H], F32)
-            for a in range(2):
-                s = 2 * pair + a
+        def grad_emb(c, half):
+            for s in (2 * half, 2 * half + 1):
+                stage = ring("stage", STAGES, [P, H], F32)
                 for oh in range(2):
                     acc = bank()
                     for g in range(2):
-                        mm(acc, ("b", c, g), slice(s * P, (s + 1) * P), ("w", c, oh, g), g == 0, g == 1)
-                    copy(engines[2 * a + oh], st[:, a * H + oh * N:a * H + (oh + 1) * N], acc[:])
-                nc.sync.dma_start(out=out_0[c].rearrange("(q s) o -> s q o", s=4)[s], in_=st[:, a * H:(a + 1) * H])
+                        mm(acc, ("dh_feat", c, g), s, ("wk", c, oh, g), g == 0, g == 1)
+                    empty_bank(False, stage[:, oh * N:(oh + 1) * N], acc[:])
+                nc.sync.dma_start(out=out_0[c].rearrange("(q s) o -> s q o", s=4)[s], in_=stage[:])
 
-        def grad_wk(c, oh, pair, engines):
-            st = ring(sb, "stage", STAGE, [P, 2 * H], F32)
-            for a in range(2):
-                k = 2 * pair + a
-                for g in range(2):
-                    acc = bank()
-                    for r in (LAB, TOK):
-                        mm(acc, ("r", c, r, oh), slice(k * P, (k + 1) * P), ("a", c, r, g), r == LAB, r == TOK)
-                    cols = st[:, a * H + g * N:a * H + (g + 1) * N]
-                    copy(engines[2 * a + g], cols.rearrange("p (m u e) -> p m u e", u=2, e=2),
-                         acc[:].rearrange("p (u m e) -> p m u e", u=2, e=2))
-                first = oh * N + k * P
-                nc.sync.dma_start(out=out_1[c, first:first + P, :], in_=st[:, a * H:(a + 1) * H])
+        def grad_wk(c, oh, half, order=BY_ROWS, vector=()):
+            stages = [ring("stage", STAGES, [P, H], F32) for a in range(2)]
+            for place, (a, g) in enumerate(order):
+                part = 2 * half + a
+                acc = bank()
+                for r in (LAB, TOK):
+                    mm(acc, ("r", c, r, oh), part, ("dh_rows", c, r, g), r == LAB, r == TOK)
+                empty_bank(place in vector,
+                           stages[a][:, g * N:(g + 1) * N].rearrange("p (m u e) -> p m u e", u=2, e=2),
+                           acc[:].rearrange("p (u m e) -> p m u e", u=2, e=2))
+                if g == 1:
+                    first = oh * N + part * P
+                    nc.sync.dma_start(out=out_1[c, first:first + P, :], in_=stages[a][:])
 
-        q = quantise
-        AAAA, AVAV, AAAV, VAVA = (A, A, A, A), (A, V, A, V), (A, A, A, V), (V, A, V, A)
-        AA, AV, VA, VAAA = (A, A), (A, V), (V, A), (V, A, A, A)
 
         load_vsum()
         load_hidden(0)
-        load_grad(0, LAB, 2)
+        load_grad(0, LAB, pieces=2)
         load_hidden(1)
         load_grad(0, TOK)
         load_wk(0, 0)
         load_wk(0, 1)
         load_emb(0)
         load_query(0, 0)
+
+        pack_hidden(0)
         load_grad(1, LAB)
         load_query(0, 1)
+        quantise("hidden", 0)
+        turn_grad(0, LAB, halves=(0,))
+        quantise("dz", 0, LAB, halves=(0,))
+        turn_grad(0, LAB, halves=(1,))
+        pack_hidden(1)
+        quantise("dz", 0, LAB, halves=(1,))
+        quantise("hidden", 1)
 
-        pack_hidden(0, (V, A))
-        q(("h", 0))
-        turn_grad(0, LAB, (0,))
-        q(("z", 0, LAB), (0,))
-        turn_grad(0, LAB, (1,))
-        q(("z", 0, LAB), (1,))
-        pack_hidden(1, (V, A))
-        q(("h", 1))
-        make_dh(0, LAB, 0, (A, A, V, A))
+        make_dh(0, LAB, 0, vector=(2,))
+        make_dh(0, LAB, 1, slices=(0, 1))
+        pack_dh(0, LAB, 0)
         turn_grad(0, TOK)
-        make_dh(0, LAB, 1, AAAA)
-        q(("z", 0, TOK))
-        pack_dh(0, LAB, 0, V)
-        turn_dh(0, 0, AA)
-        turn_wk(0, 0, 0, AA)
-        make_dh(0, TOK, 0, AAAA, (0, 1))
-        q(("a", 0, LAB, 0))
-        pack_dh(0, LAB, 1, V)
-        q(("b", 0, 0))
-        q(("w", 0, 0, 0))
-        q(("a", 0, LAB, 1))
-        turn_wk(0, 0, 1, AV)
-        make_dh(0, TOK, 0, AAAA, (2, 3))
-        turn_dh(0, 1, AA)
-        turn_wk(0, 1, 0, AA)
-        q(("w", 0, 0, 1))
-        pack_dh(0, TOK, 0, V)
-        q(("b", 0, 1))
-        make_dh(0, TOK, 1, AVAV, (0, 1))
-        turn_wk(0, 1, 1, AA)
-        q(("w", 0, 1, 0))
-        make_dh(0, TOK, 1, AAAA, (2, 3))
+        turn_dh(0, 0)
+        make_dh(0, LAB, 1, slices=(2, 3))
+        quantise("dh_rows", 0, LAB, 0)
+        quantise("dz", 0, TOK)
+        quantise("dh_feat", 0, 0)
+        pack_dh(0, LAB, 1)
+        turn_wk(0, 0, 0)
+        turn_wk(0, 0, 1, vector=(0,))
+        quantise("dh_rows", 0, LAB, 1)
+        make_dh(0, TOK, 0)
+        quantise("wk", 0, 0, 0)
+        quantise("wk", 0, 0, 1)
+        turn_dh(0, 1)
+        turn_wk(0, 1, 0)
+        pack_dh(0, TOK, 0)
+        quantise("dh_feat", 0, 1)
+        quantise("wk", 0, 1, 0)
+        make_dh(0, TOK, 1, slices=(0, 1), vector=(0,))
+        turn_wk(0, 1, 1)
+
         load_wk(1, 0)
         load_wk(1, 1)
         load_emb(1)
         load_grad(1, TOK)
         load_query(1, 0)
-        pack_r(0, LAB, 0, V)
-        q(("w", 0, 1, 1))
+        quantise("dh_rows", 0, TOK, 0)
+        quantise("wk", 0, 1, 1)
+        pack_r(0, LAB, 0)
         turn_grad(1, LAB)
-        q(("a", 0, TOK, 0))
-        q(("z", 1, LAB))
-        pack_r(0, TOK, 0, V)
+        make_dh(0, TOK, 1, slices=(2, 3))
+        quantise("r", 0, LAB, 0)
+        quantise("dz", 1, LAB)
+        pack_r(0, TOK, 0)
         load_query(1, 1)
-        grad_emb(0, 0, AAAA)
-        pack_dh(0, TOK, 1, V)
-        q(("r", 0, LAB, 0))
-        q(("r", 0, TOK, 0))
-        q(("a", 0, TOK, 1))
-        turn_wk(1, 0, 0, AA)
-        grad_emb(0, 1, AAAA)
-        make_dh(1, LAB, 0, AAAA)
-        pack_r(0, LAB, 1, V)
-        pack_r(0, TOK, 1, V)
-        q(("r", 0, LAB, 1))
-        q(("r", 0, TOK, 1))
-        turn_wk(1, 0, 1, AA)
-        grad_wk(0, 0, 0, AAAA)
-        make_dh(1, LAB, 1, AAAA)
-        q(("w", 1, 0, 0))
-        pack_dh(1, LAB, 0, V)
-        q(("w", 1, 0, 1))
-        turn_dh(1, 0, AA)
+        grad_emb(0, 0)
+        pack_dh(0, TOK, 1)
+        quantise("r", 0, TOK, 0)
+        quantise("dh_rows", 0, TOK, 1)
+        grad_emb(0, 1)
+
+        make_dh(1, LAB, 0)
+        turn_wk(1, 0, 0)
+        pack_r(0, LAB, 1)
+        pack_r(0, TOK, 1)
+        quantise("r", 0, LAB, 1)
+        quantise("r", 0, TOK, 1)
+        turn_wk(1, 0, 1)
+        grad_wk(0, 0, 0)
+        make_dh(1, LAB, 1)
+        quantise("wk", 1, 0, 0)
+        pack_dh(1, LAB, 0)
+        quantise("wk", 1, 0, 1)
+        turn_dh(1, 0)
         turn_grad(1, TOK)
-        q(("a", 1, LAB, 0))
-        grad_wk(0, 0, 1, AAAA)
-        q(("z", 1, TOK))
-        pack_dh(1, LAB, 1, V)
-        q(("b", 1, 0))
-        q(("a", 1, LAB, 1))
-        turn_dh(1, 1, AA)
-        turn_wk(1, 1, 0, AV)
-        grad_wk(0, 1, 0, AAAA)
-        q(("b", 1, 1))
-        q(("w", 1, 1, 0))
-        pack_r(1, LAB, 0, V)
-        make_dh(1, TOK, 0, (A, A, V, V))
-        turn_wk(1, 1, 1, AV)
-        grad_wk(0, 1, 1, AAAA)
-        q(("w", 1, 1, 1))
-        pack_dh(1, TOK, 0, V)
-        make_dh(1, TOK, 1, AAAA)
-        pack_r(1, TOK, 0, V)
-        q(("r", 1, LAB, 0))
-        q(("a", 1, TOK, 0))
-        q(("r", 1, TOK, 0))
-        pack_dh(1, TOK, 1, V)
-        grad_emb(1, 0, AAAA)
-        q(("a", 1, TOK, 1))
-        grad_emb(1, 1, AAAA)
-        pack_r(1, LAB, 1, V)
-        pack_r(1, TOK, 1, V)
-        q(("r", 1, LAB, 1))
-        q(("r", 1, TOK, 1))
-        grad_wk(1, 0, 0, AAAA)
-        grad_wk(1, 0, 1, (A, A, V, V))
-        grad_wk(1, 1, 0, VAVA)
-        grad_wk(1, 1, 1, VAVA)
+        quantise("dh_rows", 1, LAB, 0)
+        grad_wk(0, 0, 1)
+        quantise("dz", 1, TOK)
+        pack_dh(1, LAB, 1)
+        quantise("dh_feat", 1, 0)
+        quantise("dh_rows", 1, LAB, 1)
+        turn_dh(1, 1, vector=(1,))
+        turn_wk(1, 1, 0)
+        grad_wk(0, 1, 0)
+        pack_r(1, LAB, 0)
+        quantise("dh_feat", 1, 1)
+        quantise("wk", 1, 1, 0)
+        make_dh(1, TOK, 0, vector=(2, 3))
+        turn_wk(1, 1, 1, vector=(1,))
+        grad_wk(0, 1, 1)
+
+        quantise("wk", 1, 1, 1)
+        pack_dh(1, TOK, 0)
+        pack_r(1, TOK, 0)
+        grad_emb(1, 0)
+        quantise("r", 1, LAB, 0)
+        quantise("dh_rows", 1, TOK, 0)
+        make_dh(1, TOK, 1, vector=(0, 2))
+        quantise("r", 1, TOK, 0)
+        pack_dh(1, TOK, 1)
+        grad_emb(1, 1)
+        quantise("dh_rows", 1, TOK, 1)
+
+        for half, order, vector in ((0, BY_HALVES, ()), (1, BY_ROWS, (3,))):
+            pack_r(1, LAB, 1, halves=(half,))
+            pack_r(1, TOK, 1, halves=(half,))
+            quantise("r", 1, LAB, 1, halves=(half,))
+            quantise("r", 1, TOK, 1, halves=(half,))
+            grad_wk(1, 0, half, order, vector)
+        for half in WHOLE:
+            grad_wk(1, 1, half, vector=(0, 2))

from contextlib import ExitStack

import concourse.mybir as mybir
from concourse.masks import make_identity

C, S, F, H = 2, 512, 512, 1024
FLOPS = 2 * C * ((S + F) * S * H + F * H * H + H * (S + F) * H)
BYTES = 2 * (S * H + C * F * H + C * H * H + C * S + C * (S + F) * S) + 4 * (C * S * H + C * F * H + C * H * H)

F32 = mybir.dt.float32
BF16 = mybir.dt.bfloat16
U32 = mybir.dt.uint32
U8 = mybir.dt.uint8
E4M3 = mybir.dt.float8_e4m3fn_x4
E5M2 = mybir.dt.float8_e5m2_x4

P = 128
N = 512
HALF = N // 2
TOK, LAB = 0, 1
WHOLE = (0, 1)

BANKS = 8
PACKED = 8
DH_TILES = 4
STAGES = 12
RAW_DEPTH = {"half_mb": 4, "wk": 2, "emb": 2, "query": 3}
CODE_DEPTH = {"hidden": 2, "dz": 3, "wk": 4, "r": 8, "dh_rows": 8, "dh_feat": 2}
FORMAT = {"hidden": E4M3, "wk": E4M3, "r": E4M3, "dz": E5M2, "dh_rows": E5M2, "dh_feat": E5M2}

BY_ROWS = ((0, 0), (0, 1), (1, 0), (1, 1))
BY_HALVES = ((0, 0), (1, 0), (0, 1), (1, 1))


def tile_relationtagger_pa_v_kernel(tc, hidden, emb, Wk, Wq, vsum, query, grad_out, out_0, out_1):
    nc = tc.nc
    with ExitStack() as ctx:
        sb = ctx.enter_context(tc.tile_pool(name="sb", bufs=1))
        ps = ctx.enter_context(tc.psum_pool(name="ps", bufs=1))
        ctx.enter_context(tc.manual_schedule())

        taken = {}
        raw, packed, mx, dh = {}, {}, {}, {}
        free_slots = list(range(PACKED))
        slot_of = {}

        def ring(kind, depth, shape, dtype):
            count = taken.get(kind, 0)
            taken[kind] = count + 1
            slot = "%s%d" % (kind, count % depth)
            return sb.tile(shape, dtype, name=slot, tag=slot, align_bytes=64)

        def bank():
            count = taken.get("bank", 0)
            taken["bank"] = count + 1
            slot = "bank%d" % (count % BANKS)
            return ps.tile([P, N], F32, name=slot, tag=slot)

        def packed_tile(key):
            if key not in packed:
                slot_of[key] = free_slots.pop(0)
                slot = "packed%d" % slot_of[key]
                packed[key] = sb.tile([P, 4 * N], BF16, name=slot, tag=slot, align_bytes=64)
            return packed[key]

        def empty_bank(on_vector, out, in_):
            if on_vector:
                nc.vector.tensor_copy(out=out, in_=in_)
            else:
                nc.scalar.copy(out=out, in_=in_)

        ident = sb.tile([P, P], F32, name="ident", align_bytes=64)
        make_identity(nc, ident[:])
        vs = sb.tile([P, C, 4], BF16, name="vs", align_bytes=64)


        def load_vsum():
            nc.scalar.dma_start(out=vs[:], in_=vsum[:, 0, :].rearrange("c (p t) -> p c t", t=4))

        def load_hidden(g):
            t = ring("raw_half_mb", RAW_DEPTH["half_mb"], [P, 4 * N], BF16)
            raw["hidden", g] = t
            nc.sync.dma_start(out=t[:].rearrange("p (t h) -> p t h", t=4),
                              in_=hidden[0, :, g * N:(g + 1) * N].rearrange("(p t) h -> p t h", t=4))

        def load_grad(c, r, pieces=1):
            t = ring("raw_half_mb", RAW_DEPTH["half_mb"], [P, 4 * N], BF16)
            raw["dz", c, r] = t
            rows = grad_out[0, c, r * N:(r + 1) * N, :].rearrange("(q s) j -> q (s j)", s=4)
            width = 4 * N // pieces
            for k in range(pieces):
                nc.sync.dma_start(out=t[:, k * width:(k + 1) * width], in_=rows[:, k * width:(k + 1) * width])

        def load_wk(c, oh):
            t = ring("raw_wk", RAW_DEPTH["wk"], [P, 4 * H], BF16)
            raw["wk", c, oh] = t
            nc.sync.dma_start(out=t[:].rearrange("m (s h) -> m s h", s=4),
                              in_=Wk[c, oh * N:(oh + 1) * N, :].rearrange("(s m) h -> m s h", s=4))

        def load_emb(c):
            t = ring("raw_emb", RAW_DEPTH["emb"], [P, 4 * H], BF16)
            nc.sync.dma_start(out=t[:], in_=emb[c].rearrange("(p t) o -> p (t o)", t=4))
            for oh in range(2):
                raw["r", c, LAB, oh] = t[:].rearrange("p (t o) -> p t o", t=4)[:, :, oh * N:(oh + 1) * N]

        def load_query(c, oh):
            t = ring("raw_query", RAW_DEPTH["query"], [P, 4 * N], F32)
            nc.sync.dma_start(out=t[:].rearrange("p (t o) -> p t o", t=4),
                              in_=query[c, 0, :, oh * N:(oh + 1) * N].rearrange("(p t) o -> p t o", t=4))
            raw["r", c, TOK, oh] = t[:].rearrange("p (t o) -> p t o", t=4)


        def pack_hidden(g):
            dst = packed_tile(("hidden", g))[:].rearrange("p (u m e t) -> p u m t e", u=2, e=2, t=4)
            src = raw["hidden", g][:].rearrange("p (t m u e) -> p u m t e", t=4, u=2, e=2)
            nc.vector.tensor_copy(out=dst[:, 0], in_=src[:, 0])
            nc.scalar.copy(out=dst[:, 1], in_=src[:, 1])

        def pack(key, src, halves):
            lo, hi = halves[0] * HALF, (halves[-1] + 1) * HALF
            nc.vector.tensor_copy(
                out=packed_tile(key)[:, 4 * lo:4 * hi].rearrange("p (x i t) -> p x t i", i=4, t=4),
                in_=src[:, :, lo:hi].rearrange("p t (x i) -> p x t i", i=4))

        def pack_r(c, r, oh, halves=WHOLE):
            pack(("r", c, r, oh), raw["r", c, r, oh], halves)

        def pack_dh(c, r, g):
            pack(("dh_rows", c, r, g), dh[c, r, g][:].rearrange("p (t n) -> p t n", t=4), WHOLE)


        def turn(pairs, starts, step):
            acc = bank()
            for w in range(2):
                for s in range(2):
                    first = starts[w][s]
                    nc.tensor.transpose(acc[:, (2 * w + s) * P:(2 * w + s + 1) * P],
                                        pairs[:, first:first + (P - 1) * step + 1:step], ident[:])
            return acc

        def empty_turned(on_vector, key, half, acc):
            dst = packed_tile(key)[:].bitcast(F32)[:, half * N:(half + 1) * N]
            empty_bank(on_vector, dst.rearrange("p (n w) -> p n w", w=2), acc[:].rearrange("p (w n) -> p n w", w=2))

        def turn_grad(c, r, halves=WHOLE):
            t = packed_tile(("dz", c, r))
            pairs = raw["dz", c, r][:].bitcast(F32)
            for half in halves:
                acc = turn(pairs, [[(2 * half + s) * HALF + w for s in range(2)] for w in range(2)], 2)
                nc.vector.tensor_tensor(
                    out=t[:, half * 4 * HALF:(half + 1) * 4 * HALF].rearrange("p (n w e) -> p n w e", w=2, e=2),
                    in0=acc[:].bitcast(BF16).rearrange("p (w n e) -> p n w e", w=2, e=2),
                    in1=vs[:, c, :].rearrange("p (w e) -> p w e", e=2).unsqueeze(1).to_broadcast([P, HALF, 2, 2]),
                    op=mybir.AluOpType.mult)

        def turn_wk(c, oh, g, vector=()):
            packed_tile(("wk", c, oh, g))
            pairs = raw["wk", c, oh][:].bitcast(F32)
            for half in WHOLE:
                acc = turn(pairs, [[(2 * half + s) * N + g * HALF + w for s in range(2)] for w in range(2)], 2)
                empty_turned(half in vector, ("wk", c, oh, g), half, acc)

        def turn_dh(c, g, vector=()):
            packed_tile(("dh_feat", c, g))
            pairs = dh[c, LAB, g][:].bitcast(F32)
            for half in WHOLE:
                acc = turn(pairs, [[(2 * half + s) * HALF + w * P for s in range(2)] for w in range(2)], 1)
                empty_turned(half in vector, ("dh_feat", c, g), half, acc)


        def quantise(*key, halves=WHOLE):
            kind = key[0]
            if key not in mx:
                codes = ring("codes_" + kind, CODE_DEPTH[kind], [P, N], U32)
                scales = ring("scales_" + kind, CODE_DEPTH[kind], [P, N], U8)
                mx[key] = (codes[:].bitcast(FORMAT[kind]), scales)
            lo, hi = halves[0] * HALF, (halves[-1] + 1) * HALF
            nc.vector.quantize_mx(out=mx[key][0][:, lo:hi], scales=mx[key][1][:, lo:hi],
                                  in_=packed[key][:, 4 * lo:4 * hi])
            if halves[-1] == WHOLE[-1]:
                free_slots.append(slot_of[key])

        def mm(acc, left, part, right, start, stop):
            cols = slice(part * P, (part + 1) * P)
            nc.tensor.matmul_mx(out=acc[:], lhsT=mx[left][0][:, cols], lhsT_scale=mx[left][1][:, cols],
                                rhs=mx[right][0], rhs_scale=mx[right][1][:], start=start, stop=stop)

        def make_dh(c, r, g, slices=(0, 1, 2, 3), vector=()):
            if (c, r, g) not in dh:
                dh[c, r, g] = ring("dh", DH_TILES, [P, 4 * N], BF16)
            for s in slices:
                acc = bank()
                mm(acc, ("dz", c, r), s, ("hidden", g), True, True)
                empty_bank(s in vector, dh[c, r, g][:, s * N:(s + 1) * N], acc[:])

        def grad_emb(c, half):
            for s in (2 * half, 2 * half + 1):
                stage = ring("stage", STAGES, [P, H], F32)
                for oh in range(2):
                    acc = bank()
                    for g in range(2):
                        mm(acc, ("dh_feat", c, g), s, ("wk", c, oh, g), g == 0, g == 1)
                    empty_bank(False, stage[:, oh * N:(oh + 1) * N], acc[:])
                nc.sync.dma_start(out=out_0[c].rearrange("(q s) o -> s q o", s=4)[s], in_=stage[:])

        def grad_wk(c, oh, half, order=BY_ROWS, vector=()):
            stages = [ring("stage", STAGES, [P, H], F32) for a in range(2)]
            for place, (a, g) in enumerate(order):
                part = 2 * half + a
                acc = bank()
                for r in (LAB, TOK):
                    mm(acc, ("r", c, r, oh), part, ("dh_rows", c, r, g), r == LAB, r == TOK)
                empty_bank(place in vector,
                           stages[a][:, g * N:(g + 1) * N].rearrange("p (m u e) -> p m u e", u=2, e=2),
                           acc[:].rearrange("p (u m e) -> p m u e", u=2, e=2))
                if g == 1:
                    first = oh * N + part * P
                    nc.sync.dma_start(out=out_1[c, first:first + P, :], in_=stages[a][:])


        load_vsum()
        load_hidden(0)
        load_grad(0, LAB, pieces=2)
        load_hidden(1)
        load_grad(0, TOK)
        load_wk(0, 0)
        load_wk(0, 1)
        load_emb(0)
        load_query(0, 0)

        pack_hidden(0)
        load_grad(1, LAB)
        load_query(0, 1)
        quantise("hidden", 0)
        turn_grad(0, LAB, halves=(0,))
        quantise("dz", 0, LAB, halves=(0,))
        turn_grad(0, LAB, halves=(1,))
        pack_hidden(1)
        quantise("dz", 0, LAB, halves=(1,))
        quantise("hidden", 1)

        make_dh(0, LAB, 0, vector=(2,))
        make_dh(0, LAB, 1, slices=(0, 1))
        pack_dh(0, LAB, 0)
        turn_grad(0, TOK)
        turn_dh(0, 0)
        make_dh(0, LAB, 1, slices=(2, 3))
        quantise("dh_rows", 0, LAB, 0)
        quantise("dz", 0, TOK)
        quantise("dh_feat", 0, 0)
        pack_dh(0, LAB, 1)
        turn_wk(0, 0, 0)
        turn_wk(0, 0, 1, vector=(0,))
        quantise("dh_rows", 0, LAB, 1)
        make_dh(0, TOK, 0)
        quantise("wk", 0, 0, 0)
        quantise("wk", 0, 0, 1)
        turn_dh(0, 1)
        turn_wk(0, 1, 0)
        pack_dh(0, TOK, 0)
        quantise("dh_feat", 0, 1)
        quantise("wk", 0, 1, 0)
        make_dh(0, TOK, 1, slices=(0, 1), vector=(0,))
        turn_wk(0, 1, 1)

        load_wk(1, 0)
        load_wk(1, 1)
        load_emb(1)
        load_grad(1, TOK)
        load_query(1, 0)
        quantise("dh_rows", 0, TOK, 0)
        quantise("wk", 0, 1, 1)
        pack_r(0, LAB, 0)
        turn_grad(1, LAB)
        make_dh(0, TOK, 1, slices=(2, 3))
        quantise("r", 0, LAB, 0)
        quantise("dz", 1, LAB)
        pack_r(0, TOK, 0)
        load_query(1, 1)
        grad_emb(0, 0)
        pack_dh(0, TOK, 1)
        quantise("r", 0, TOK, 0)
        quantise("dh_rows", 0, TOK, 1)
        grad_emb(0, 1)

        make_dh(1, LAB, 0)
        turn_wk(1, 0, 0)
        pack_r(0, LAB, 1)
        pack_r(0, TOK, 1)
        quantise("r", 0, LAB, 1)
        quantise("r", 0, TOK, 1)
        turn_wk(1, 0, 1)
        grad_wk(0, 0, 0)
        make_dh(1, LAB, 1)
        quantise("wk", 1, 0, 0)
        pack_dh(1, LAB, 0)
        quantise("wk", 1, 0, 1)
        turn_dh(1, 0)
        turn_grad(1, TOK)
        quantise("dh_rows", 1, LAB, 0)
        grad_wk(0, 0, 1)
        quantise("dz", 1, TOK)
        pack_dh(1, LAB, 1)
        quantise("dh_feat", 1, 0)
        quantise("dh_rows", 1, LAB, 1)
        turn_dh(1, 1, vector=(1,))
        turn_wk(1, 1, 0)
        grad_wk(0, 1, 0)
        pack_r(1, LAB, 0)
        quantise("dh_feat", 1, 1)
        quantise("wk", 1, 1, 0)
        make_dh(1, TOK, 0, vector=(2, 3))
        turn_wk(1, 1, 1, vector=(1,))
        grad_wk(0, 1, 1)

        quantise("wk", 1, 1, 1)
        pack_dh(1, TOK, 0)
        pack_r(1, TOK, 0)
        grad_emb(1, 0)
        quantise("r", 1, LAB, 0)
        quantise("dh_rows", 1, TOK, 0)
        make_dh(1, TOK, 1, vector=(0, 2))
        quantise("r", 1, TOK, 0)
        pack_dh(1, TOK, 1)
        grad_emb(1, 1)
        quantise("dh_rows", 1, TOK, 1)

        for half, order, vector in ((0, BY_HALVES, ()), (1, BY_ROWS, (3,))):
            pack_r(1, LAB, 1, halves=(half,))
            pack_r(1, TOK, 1, halves=(half,))
            quantise("r", 1, LAB, 1, halves=(half,))
            quantise("r", 1, TOK, 1, halves=(half,))
            grad_wk(1, 0, half, order, vector)
        for half in WHOLE:
            grad_wk(1, 1, half, vector=(0, 2))
